import numpy as np
import ml_dtypes


def mxq(x, axis, fmt="e4m3"):
    dtype, down = {"e4m3": (ml_dtypes.float8_e4m3fn, 7), "e5m2": (ml_dtypes.float8_e5m2, 14)}[fmt]
    v = np.moveaxis(np.asarray(x, np.float32).astype(ml_dtypes.bfloat16).astype(np.float64), axis, -1)
    blocks = v.reshape(v.shape[:-1] + (-1, 32))
    amax = np.abs(blocks).max(-1, keepdims=True)
    byte = np.maximum(np.where(amax > 0, np.frexp(amax)[1] - 1 + 127, 0) - down, 1)
    scale = np.exp2(byte - 127.0)
    codes = (blocks / scale).astype(np.float32).astype(dtype).astype(np.float64)
    return np.moveaxis((codes * scale).reshape(v.shape), -1, axis)


WIDE = False


def mx_kscale(k):
    if not WIDE:
        return np.ones(k)
    levels = np.array([10, -10, 5, -5, 0])
    a = np.random.permutation(np.resize(levels, k // 512 * 4)).reshape(k // 512, 4)
    idx = np.arange(k)
    return np.exp2(a[idx // 512, idx % 128 // 32])


BF16 = ml_dtypes.bfloat16


def bf(x):
    return np.asarray(x, np.float32).astype(BF16)


def f64(x):
    return np.asarray(x).astype(np.float64)


B, T, C, H, NOPE, ROPE, VD, LORA = 1, 512, 2048, 16, 128, 128, 128, 512
QK = NOPE + ROPE
HALF = ROPE // 2


def make_freq_cis():
    inv = 1.0 / (10000.0 ** (np.arange(0, ROPE, 2) / ROPE))
    ang = np.outer(np.arange(T), inv)
    return np.stack([np.cos(ang), np.sin(ang)], -1)


def apply_rope(v, fc):
    vr = v.reshape(B, T, H, HALF, 2)
    f = fc.reshape(1, T, 1, HALF, 2)
    real = vr[..., 0] * f[..., 0] - vr[..., 1] * f[..., 1]
    imag = vr[..., 1] * f[..., 0] + vr[..., 0] * f[..., 1]
    return np.stack([real, imag], -1).reshape(B, T, H, ROPE)


def setup_inputs():
    s = mx_kscale(C)
    return {"x": bf(np.random.standard_normal((B, T, C)) * s),
            "freq_cis": bf(make_freq_cis()),
            "Wq": bf(np.random.standard_normal((C, H * QK)) * 2.0 / np.sqrt(C) / s[:, None])}


def reference(x, freq_cis, Wq):
    q = (mxq(f64(x), 2, "e4m3") @ mxq(f64(Wq), 0, "e4m3")).reshape(B, T, H, QK)
    q_nope, q_rope = q[..., :NOPE], q[..., NOPE:]
    q_rope = apply_rope(q_rope, f64(freq_cis))
    return np.concatenate([q_nope, q_rope], -1)

@@ -1,0 +1,219 @@
+from contextlib import ExitStack
+
+import concourse.mybir as mybir
+from concourse.masks import make_identity
+
+FLOPS = 2 * 512 * 2048 * 4096
+
+BF16 = mybir.dt.bfloat16
+F32 = mybir.dt.float32
+U32 = mybir.dt.uint32
+U8 = mybir.dt.uint8
+FP8X4 = mybir.dt.float8_e4m3fn_x4
+MULT = mybir.AluOpType.mult
+ADD = mybir.AluOpType.add
+
+P = 128
+PACK = 4
+K_PASS = P * PACK
+TOKENS = 512
+K = 2048
+PASSES = K // K_PASS
+TOK_TILES = TOKENS // P
+HEAD = 256
+HALF = 128
+PAIRS = HALF // 2
+BLOCK_HEADS = 4
+BLOCK = BLOCK_HEADS * HEAD
+BANK = BLOCK_HEADS * HALF
+BLOCKS = 4096 // BLOCK
+UNITS = BLOCKS * PASSES
+KEPT, ROTATED = 0, 1
+PIECES = 2 * BLOCK_HEADS
+VECTOR_PIECES = 3
+
+
+def tile_multiheadlatentattention_pb_kernel(tc, x, freq_cis, Wq, out):
+    nc = tc.nc
+    x_tiles = x.rearrange("b (tt p) c -> (b tt) p c", p=P)
+    out_tiles = out.rearrange("b (tt p) h d -> (b tt) p (h d)", p=P)
+
+    with ExitStack() as ctx:
+        keep = ctx.enter_context(tc.tile_pool(name="keep", bufs=1))
+        raw_pool = ctx.enter_context(tc.tile_pool(name="raw", bufs=UNITS))
+        grouped_pool = ctx.enter_context(tc.tile_pool(name="grouped", bufs=3))
+        codes_pool = ctx.enter_context(tc.tile_pool(name="codes", bufs=3))
+        psum = ctx.enter_context(tc.psum_pool(name="psum", bufs=1))
+
+        def bank(index, shape, name):
+            return psum.tile(shape, F32, name=name, tag="bank%d" % index)
+
+        ident = keep.tile([P, P], F32, name="ident")
+        make_identity(nc, ident[:])
+
+        freq_raw = keep.tile([P, TOK_TILES, PAIRS, 2], BF16, name="freq_raw")
+        nc.scalar.dma_start(
+            out=freq_raw[:], in_=freq_cis.rearrange("(tt p) i two -> p tt i two", p=P)
+        )
+        cos_sin = keep.tile([P, TOK_TILES, PAIRS, 2], F32, name="cos_sin")
+        negsin_cos = keep.tile([P, TOK_TILES, PAIRS, 2], F32, name="negsin_cos")
+        nc.vector.tensor_copy(out=cos_sin[:], in_=freq_raw[:])
+        nc.vector.tensor_scalar_mul(
+            out=negsin_cos[:, :, :, 0:1], in0=freq_raw[:, :, :, 1:2], scalar1=-1.0
+        )
+        nc.vector.tensor_copy(out=negsin_cos[:, :, :, 1:2], in_=freq_raw[:, :, :, 0:1])
+
+        w_raw = [
+            raw_pool.tile([P, PACK, BLOCK], BF16, name="w_raw") for n in range(UNITS)
+        ]
+
+        def load_weights(n):
+            b, g = divmod(n, PASSES)
+            for u in range(2):
+                first = K_PASS * g + 2 * P * u
+                rows = Wq[first : first + 2 * P, BLOCK * b : BLOCK * (b + 1)]
+                nc.sync.dma_start(
+                    out=w_raw[n][:, 2 * u : 2 * u + 2, :],
+                    in_=rows.rearrange("(q e) c -> q e c", e=2),
+                )
+
+        w_grouped = {}
+        w_codes = {}
+        w_scales = {}
+        acc = {}
+
+        def regroup(n):
+            w_grouped[n] = grouped_pool.tile(
+                [P, BLOCK, PACK], BF16, name="w_grouped", align_bytes=64
+            )
+            for piece in range(PIECES):
+                kind, h = divmod(piece, BLOCK_HEADS)
+                src = w_raw[n][:, :, HEAD * h + HALF * kind : HEAD * h + HALF * (kind + 1)]
+                dst = w_grouped[n][:, HALF * piece : HALF * (piece + 1), :]
+                if piece < PIECES - VECTOR_PIECES:
+                    copy = nc.scalar.copy
+                else:
+                    copy = nc.vector.tensor_copy
+                copy(
+                    out=dst.rearrange("p (c i) t -> p c t i", i=4),
+                    in_=src.rearrange("p t (c i) -> p c t i", i=4),
+                )
+
+        def quantise(n):
+            w_codes[n] = codes_pool.tile([P, 2, BANK], U32, name="w_codes", align_bytes=64)
+            w_scales[n] = codes_pool.tile([P, 2, BANK], U8, name="w_scales", align_bytes=64)
+            for kind in (KEPT, ROTATED):
+                nc.vector.quantize_mx(
+                    out=w_codes[n][:, kind, :].bitcast(FP8X4),
+                    scales=w_scales[n][:, kind, :],
+                    in_=w_grouped[n][:, BANK * kind : BANK * (kind + 1), :].rearrange(
+                        "p w t -> p (w t)"
+                    ),
+                )
+
+        def multiply(n):
+            g = n % PASSES
+            for kind in (KEPT, ROTATED):
+                for tt in range(TOK_TILES):
+                    if g == 0:
+                        acc[kind, tt] = bank(TOK_TILES * kind + tt, [P, BANK], "acc")
+                    nc.tensor.matmul_mx(
+                        out=acc[kind, tt][:],
+                        lhsT=x_codes[:, tt, P * g : P * (g + 1)].bitcast(FP8X4),
+                        lhsT_scale=x_scales[:, tt, P * g : P * (g + 1)],
+                        rhs=w_codes[n][:, kind, :].bitcast(FP8X4),
+                        rhs_scale=w_scales[n][:, kind, :],
+                        start=(g == 0),
+                        stop=(g == PASSES - 1),
+                    )
+
+        x_codes = keep.tile([P, TOK_TILES, PASSES * P], U32, name="x_codes", align_bytes=64)
+        x_scales = keep.tile([P, TOK_TILES, PASSES * P], U8, name="x_scales", align_bytes=64)
+        with tc.tile_pool(name="x", bufs=TOK_TILES) as x_pool:
+            x_raw = [x_pool.tile([P, K], BF16, name="x_raw") for tt in range(TOK_TILES)]
+            load_weights(0)
+            for tt in range(TOK_TILES):
+                nc.sync.dma_start(out=x_raw[tt][:], in_=x_tiles[tt])
+            for n in range(1, UNITS):
+                load_weights(n)
+
+            regroup(0)
+
+            for tt in range(TOK_TILES):
+                x_words = x_raw[tt][:].bitcast(F32)
+                x_grouped = x_pool.tile([P, K], BF16, name="x_grouped", align_bytes=64)
+                grouped_words = x_grouped[:].bitcast(F32).rearrange(
+                    "p (g r u) -> p g r u", g=PASSES, u=2
+                )
+                for half in range(2):
+                    xt = bank(2 * tt + half, [P, 2, 2, P], "xt")
+                    for g2 in range(2):
+                        for u in range(2):
+                            first = P * (2 * (2 * half + g2) + u)
+                            nc.tensor.transpose(
+                                xt[:, g2, u, :], x_words[:, first : first + P], ident[:]
+                            )
+                    copy = nc.scalar.copy if half == 0 else nc.vector.tensor_copy
+                    copy(
+                        out=grouped_words[:, 2 * half : 2 * half + 2, :, :],
+                        in_=xt[:].rearrange("p g u r -> p g r u"),
+                    )
+                nc.vector.quantize_mx(
+                    out=x_codes[:, tt, :].bitcast(FP8X4),
+                    scales=x_scales[:, tt, :],
+                    in_=x_grouped[:],
+                )
+
+        stage_pool = ctx.enter_context(tc.tile_pool(name="stage", bufs=6))
+        rope_pool = ctx.enter_context(tc.tile_pool(name="rope", bufs=2))
+        rot_shape = [P, BLOCK_HEADS, PAIRS, 2]
+
+        def evacuate(b):
+            stage = {}
+            from_even = {}
+            from_odd = {}
+            for tt in range(TOK_TILES + 1):
+                if tt < TOK_TILES:
+                    stage[tt] = stage_pool.tile([P, BLOCK_HEADS, 2, HALF], F32, name="stage")
+                    nc.scalar.copy(
+                        out=stage[tt][:, :, KEPT, :],
+                        in_=acc[KEPT, tt][:].rearrange("p (h f) -> p h f", h=BLOCK_HEADS),
+                    )
+                    pairs = acc[ROTATED, tt][:].rearrange(
+                        "p (h i two) -> p h i two", h=BLOCK_HEADS, two=2
+                    )
+                    from_even[tt] = rope_pool.tile(rot_shape, F32, name="from_even")
+                    from_odd[tt] = rope_pool.tile(rot_shape, F32, name="from_odd")
+                    nc.vector.tensor_tensor(
+                        out=from_even[tt][:],
+                        in0=pairs[:, :, :, 0:1].to_broadcast(rot_shape),
+                        in1=cos_sin[:, tt : tt + 1, :, :].to_broadcast(rot_shape),
+                        op=MULT,
+                    )
+                    nc.vector.tensor_tensor(
+                        out=from_odd[tt][:],
+                        in0=pairs[:, :, :, 1:2].to_broadcast(rot_shape),
+                        in1=negsin_cos[:, tt : tt + 1, :, :].to_broadcast(rot_shape),
+                        op=MULT,
+                    )
+                if tt >= 1:
+                    done = tt - 1
+                    nc.vector.tensor_tensor(
+                        out=stage[done][:, :, ROTATED, :],
+                        in0=from_even[done][:].rearrange("p h i two -> p h (i two)"),
+                        in1=from_odd[done][:].rearrange("p h i two -> p h (i two)"),
+                        op=ADD,
+                    )
+                    nc.sync.dma_start(
+                        out=out_tiles[done][:, BLOCK * b : BLOCK * (b + 1)],
+                        in_=stage[done][:].rearrange("p h s f -> p (h s f)"),
+                    )
+
+        for n in range(UNITS):
+            if n + 1 < UNITS:
+                regroup(n + 1)
+            quantise(n)
+            if n >= PASSES and n % PASSES == 0:
+                evacuate(n // PASSES - 1)
+            multiply(n)
+        evacuate(BLOCKS - 1)

@@ -27,10 +27,10 @@ BLOCK_HEADS = 4
 BLOCK = BLOCK_HEADS * HEAD
 BANK = BLOCK_HEADS * HALF
 BLOCKS = 4096 // BLOCK
-UNITS = BLOCKS * PASSES
-KEPT, ROTATED = 0, 1
-PIECES = 2 * BLOCK_HEADS
-VECTOR_PIECES = 3
+ROTATED, KEPT = 0, 1
+GROUPS = 2 * BLOCKS
+UNITS = GROUPS * PASSES
+VECTOR_HEADS = {ROTATED: 2, KEPT: 1}
 
 
 def tile_multiheadlatentattention_pb_kernel(tc, x, freq_cis, Wq, out):
@@ -39,10 +39,11 @@ def tile_multiheadlatentattention_pb_kernel(tc, x, freq_cis, Wq, out):
     out_tiles = out.rearrange("b (tt p) h d -> (b tt) p (h d)", p=P)
 
     with ExitStack() as ctx:
+        ctx.enter_context(tc.manual_schedule())
         keep = ctx.enter_context(tc.tile_pool(name="keep", bufs=1))
-        raw_pool = ctx.enter_context(tc.tile_pool(name="raw", bufs=UNITS))
-        grouped_pool = ctx.enter_context(tc.tile_pool(name="grouped", bufs=3))
-        codes_pool = ctx.enter_context(tc.tile_pool(name="codes", bufs=3))
+        raw_pool = ctx.enter_context(tc.tile_pool(name="raw", bufs=BLOCKS * PASSES))
+        grouped_pool = ctx.enter_context(tc.tile_pool(name="grouped", bufs=4))
+        codes_pool = ctx.enter_context(tc.tile_pool(name="codes", bufs=4))
         psum = ctx.enter_context(tc.psum_pool(name="psum", bufs=1))
 
         def bank(index, shape, name):
@@ -63,81 +64,24 @@ def tile_multiheadlatentattention_pb_kernel(tc, x, freq_cis, Wq, out):
         )
         nc.vector.tensor_copy(out=negsin_cos[:, :, :, 1:2], in_=freq_raw[:, :, :, 0:1])
 
-        w_raw = [
-            raw_pool.tile([P, PACK, BLOCK], BF16, name="w_raw") for n in range(UNITS)
-        ]
-
-        def load_weights(n):
-            b, g = divmod(n, PASSES)
-            for u in range(2):
-                first = K_PASS * g + 2 * P * u
-                rows = Wq[first : first + 2 * P, BLOCK * b : BLOCK * (b + 1)]
-                nc.sync.dma_start(
-                    out=w_raw[n][:, 2 * u : 2 * u + 2, :],
-                    in_=rows.rearrange("(q e) c -> q e c", e=2),
-                )
-
-        w_grouped = {}
-        w_codes = {}
-        w_scales = {}
-        acc = {}
-
-        def regroup(n):
-            w_grouped[n] = grouped_pool.tile(
-                [P, BLOCK, PACK], BF16, name="w_grouped", align_bytes=64
-            )
-            for piece in range(PIECES):
-                kind, h = divmod(piece, BLOCK_HEADS)
-                src = w_raw[n][:, :, HEAD * h + HALF * kind : HEAD * h + HALF * (kind + 1)]
-                dst = w_grouped[n][:, HALF * piece : HALF * (piece + 1), :]
-                if piece < PIECES - VECTOR_PIECES:
-                    copy = nc.scalar.copy
-                else:
-                    copy = nc.vector.tensor_copy
-                copy(
-                    out=dst.rearrange("p (c i) t -> p c t i", i=4),
-                    in_=src.rearrange("p t (c i) -> p c t i", i=4),
-                )
-
-        def quantise(n):
-            w_codes[n] = codes_pool.tile([P, 2, BANK], U32, name="w_codes", align_bytes=64)
-            w_scales[n] = codes_pool.tile([P, 2, BANK], U8, name="w_scales", align_bytes=64)
-            for kind in (KEPT, ROTATED):
-                nc.vector.quantize_mx(
-                    out=w_codes[n][:, kind, :].bitcast(FP8X4),
-                    scales=w_scales[n][:, kind, :],
-                    in_=w_grouped[n][:, BANK * kind : BANK * (kind + 1), :].rearrange(
-                        "p w t -> p (w t)"
-                    ),
-                )
-
-        def multiply(n):
-            g = n % PASSES
-            for kind in (KEPT, ROTATED):
-                for tt in range(TOK_TILES):
-                    if g == 0:
-                        acc[kind, tt] = bank(TOK_TILES * kind + tt, [P, BANK], "acc")
-                    nc.tensor.matmul_mx(
-                        out=acc[kind, tt][:],
-                        lhsT=x_codes[:, tt, P * g : P * (g + 1)].bitcast(FP8X4),
-                        lhsT_scale=x_scales[:, tt, P * g : P * (g + 1)],
-                        rhs=w_codes[n][:, kind, :].bitcast(FP8X4),
-                        rhs_scale=w_scales[n][:, kind, :],
-                        start=(g == 0),
-                        stop=(g == PASSES - 1),
-                    )
-
         x_codes = keep.tile([P, TOK_TILES, PASSES * P], U32, name="x_codes", align_bytes=64)
         x_scales = keep.tile([P, TOK_TILES, PASSES * P], U8, name="x_scales", align_bytes=64)
+        w_raw = {}
         with tc.tile_pool(name="x", bufs=TOK_TILES) as x_pool:
             x_raw = [x_pool.tile([P, K], BF16, name="x_raw") for tt in range(TOK_TILES)]
-            load_weights(0)
             for tt in range(TOK_TILES):
                 nc.sync.dma_start(out=x_raw[tt][:], in_=x_tiles[tt])
-            for n in range(1, UNITS):
-                load_weights(n)
 
-            regroup(0)
+            for b in range(BLOCKS):
+                for g in range(PASSES):
+                    w_raw[b, g] = raw_pool.tile([P, PACK, BLOCK], BF16, name="w_raw")
+                    for u in range(2):
+                        first = K_PASS * g + 2 * P * u
+                        rows = Wq[first : first + 2 * P, BLOCK * b : BLOCK * (b + 1)]
+                        nc.sync.dma_start(
+                            out=w_raw[b, g][:, 2 * u : 2 * u + 2, :],
+                            in_=rows.rearrange("(q e) c -> q e c", e=2),
+                        )
 
             for tt in range(TOK_TILES):
                 x_words = x_raw[tt][:].bitcast(F32)
@@ -164,56 +108,102 @@ def tile_multiheadlatentattention_pb_kernel(tc, x, freq_cis, Wq, out):
                     in_=x_grouped[:],
                 )
 
-        stage_pool = ctx.enter_context(tc.tile_pool(name="stage", bufs=6))
-        rope_pool = ctx.enter_context(tc.tile_pool(name="rope", bufs=2))
+        stage_pool = ctx.enter_context(tc.tile_pool(name="stage", bufs=2 * TOK_TILES))
+        rope_pool = ctx.enter_context(tc.tile_pool(name="rope", bufs=3))
         rot_shape = [P, BLOCK_HEADS, PAIRS, 2]
+        w_grouped = {}
+        w_codes = {}
+        w_scales = {}
+        acc = {}
+        stage = {}
 
-        def evacuate(b):
-            stage = {}
-            from_even = {}
-            from_odd = {}
-            for tt in range(TOK_TILES + 1):
-                if tt < TOK_TILES:
-                    stage[tt] = stage_pool.tile([P, BLOCK_HEADS, 2, HALF], F32, name="stage")
-                    nc.scalar.copy(
-                        out=stage[tt][:, :, KEPT, :],
-                        in_=acc[KEPT, tt][:].rearrange("p (h f) -> p h f", h=BLOCK_HEADS),
-                    )
-                    pairs = acc[ROTATED, tt][:].rearrange(
-                        "p (h i two) -> p h i two", h=BLOCK_HEADS, two=2
-                    )
-                    from_even[tt] = rope_pool.tile(rot_shape, F32, name="from_even")
-                    from_odd[tt] = rope_pool.tile(rot_shape, F32, name="from_odd")
-                    nc.vector.tensor_tensor(
-                        out=from_even[tt][:],
-                        in0=pairs[:, :, :, 0:1].to_broadcast(rot_shape),
-                        in1=cos_sin[:, tt : tt + 1, :, :].to_broadcast(rot_shape),
-                        op=MULT,
-                    )
-                    nc.vector.tensor_tensor(
-                        out=from_odd[tt][:],
-                        in0=pairs[:, :, :, 1:2].to_broadcast(rot_shape),
-                        in1=negsin_cos[:, tt : tt + 1, :, :].to_broadcast(rot_shape),
-                        op=MULT,
-                    )
-                if tt >= 1:
-                    done = tt - 1
-                    nc.vector.tensor_tensor(
-                        out=stage[done][:, :, ROTATED, :],
-                        in0=from_even[done][:].rearrange("p h i two -> p h (i two)"),
-                        in1=from_odd[done][:].rearrange("p h i two -> p h (i two)"),
-                        op=ADD,
-                    )
-                    nc.sync.dma_start(
-                        out=out_tiles[done][:, BLOCK * b : BLOCK * (b + 1)],
-                        in_=stage[done][:].rearrange("p h s f -> p (h s f)"),
-                    )
+        def regroup(n):
+            group, g = divmod(n, PASSES)
+            b, kind = divmod(group, 2)
+            w_grouped[n] = grouped_pool.tile(
+                [P, BANK, PACK], BF16, name="w_grouped", align_bytes=64
+            )
+            for h in range(BLOCK_HEADS):
+                first = HEAD * h + (HALF if kind == ROTATED else 0)
+                src = w_raw[b, g][:, :, first : first + HALF]
+                dst = w_grouped[n][:, HALF * h : HALF * (h + 1), :]
+                if h < BLOCK_HEADS - VECTOR_HEADS[kind]:
+                    copy = nc.scalar.copy
+                else:
+                    copy = nc.vector.tensor_copy
+                copy(
+                    out=dst.rearrange("p (c i) t -> p c t i", i=4),
+                    in_=src.rearrange("p t (c i) -> p c t i", i=4),
+                )
 
+        def quantise(n):
+            w_codes[n] = codes_pool.tile([P, BANK], U32, name="w_codes", align_bytes=64)
+            w_scales[n] = codes_pool.tile([P, BANK], U8, name="w_scales", align_bytes=64)
+            nc.vector.quantize_mx(
+                out=w_codes[n][:].bitcast(FP8X4),
+                scales=w_scales[n][:],
+                in_=w_grouped[n][:].rearrange("p w t -> p (w t)"),
+            )
+
+        def multiply(n):
+            group, g = divmod(n, PASSES)
+            for tt in range(TOK_TILES):
+                if g == 0:
+                    acc[group, tt] = bank(TOK_TILES * (group % 2) + tt, [P, BANK], "acc")
+                nc.tensor.matmul_mx(
+                    out=acc[group, tt][:],
+                    lhsT=x_codes[:, tt, P * g : P * (g + 1)].bitcast(FP8X4),
+                    lhsT_scale=x_scales[:, tt, P * g : P * (g + 1)],
+                    rhs=w_codes[n][:].bitcast(FP8X4),
+                    rhs_scale=w_scales[n][:],
+                    start=(g == 0),
+                    stop=(g == PASSES - 1),
+                )
+
+        def evacuate(group, tt):
+            b, kind = divmod(group, 2)
+            if kind == ROTATED:
+                stage[b, tt] = stage_pool.tile([P, BLOCK_HEADS, 2, HALF], F32, name="stage")
+                pairs = acc[group, tt][:].rearrange(
+                    "p (h i two) -> p h i two", h=BLOCK_HEADS, two=2
+                )
+                from_even = rope_pool.tile(rot_shape, F32, name="from_even")
+                from_odd = rope_pool.tile(rot_shape, F32, name="from_odd")
+                nc.vector.tensor_tensor(
+                    out=from_even[:],
+                    in0=pairs[:, :, :, 0:1].to_broadcast(rot_shape),
+                    in1=cos_sin[:, tt : tt + 1, :, :].to_broadcast(rot_shape),
+                    op=MULT,
+                )
+                nc.vector.tensor_tensor(
+                    out=from_odd[:],
+                    in0=pairs[:, :, :, 1:2].to_broadcast(rot_shape),
+                    in1=negsin_cos[:, tt : tt + 1, :, :].to_broadcast(rot_shape),
+                    op=MULT,
+                )
+                nc.gpsimd.tensor_tensor(
+                    out=stage[b, tt][:, :, 1, :],
+                    in0=from_even[:].rearrange("p h i two -> p h (i two)"),
+                    in1=from_odd[:].rearrange("p h i two -> p h (i two)"),
+                    op=ADD,
+                )
+            else:
+                nc.scalar.copy(
+                    out=stage[b, tt][:, :, 0, :],
+                    in_=acc[group, tt][:].rearrange("p (h f) -> p h f", h=BLOCK_HEADS),
+                )
+                nc.sync.dma_start(
+                    out=out_tiles[tt][:, BLOCK * b : BLOCK * (b + 1)],
+                    in_=stage[b, tt][:].rearrange("p h s f -> p (h s f)"),
+                )
+
+        regroup(0)
         for n in range(UNITS):
             if n + 1 < UNITS:
                 regroup(n + 1)
             quantise(n)
-            if n >= PASSES and n % PASSES == 0:
-                evacuate(n // PASSES - 1)
+            if n >= PASSES:
+                evacuate(n // PASSES - 1, n % PASSES)
             multiply(n)
-        evacuate(BLOCKS - 1)
+        for tt in range(TOK_TILES):
+            evacuate(GROUPS - 1, tt)

@@ -123,18 +123,13 @@ def tile_multiheadlatentattention_pb_kernel(tc, x, freq_cis, Wq, out):
             w_grouped[n] = grouped_pool.tile(
                 [P, BANK, PACK], BF16, name="w_grouped", align_bytes=64
             )
-            for h in range(BLOCK_HEADS):
-                first = HEAD * h + (HALF if kind == ROTATED else 0)
-                src = w_raw[b, g][:, :, first : first + HALF]
-                dst = w_grouped[n][:, HALF * h : HALF * (h + 1), :]
-                if h < BLOCK_HEADS - VECTOR_HEADS[kind]:
-                    copy = nc.scalar.copy
-                else:
-                    copy = nc.vector.tensor_copy
-                copy(
-                    out=dst.rearrange("p (c i) t -> p c t i", i=4),
-                    in_=src.rearrange("p t (c i) -> p c t i", i=4),
-                )
+            src = w_raw[b, g][:].rearrange(
+                "p t (h s c i) -> p s h c t i", h=BLOCK_HEADS, s=2, i=4
+            )[:, 1 if kind == ROTATED else 0]
+            dst = w_grouped[n][:].rearrange("p (h c i) t -> p h c t i", h=BLOCK_HEADS, i=4)
+            split = BLOCK_HEADS - VECTOR_HEADS[kind]
+            nc.scalar.copy(out=dst[:, :split], in_=src[:, :split])
+            nc.vector.tensor_copy(out=dst[:, split:], in_=src[:, split:])
 
         def quantise(n):
             w_codes[n] = codes_pool.tile([P, BANK], U32, name="w_codes", align_bytes=64)

@@ -30,6 +30,7 @@ BLOCKS = 4096 // BLOCK
 ROTATED, KEPT = 0, 1
 GROUPS = 2 * BLOCKS
 UNITS = GROUPS * PASSES
+LEAVE_LAG = PASSES + 1
 VECTOR_HEADS = {ROTATED: 2, KEPT: 1}
 
 
@@ -42,8 +43,8 @@ def tile_multiheadlatentattention_pb_kernel(tc, x, freq_cis, Wq, out):
         ctx.enter_context(tc.manual_schedule())
         keep = ctx.enter_context(tc.tile_pool(name="keep", bufs=1))
         raw_pool = ctx.enter_context(tc.tile_pool(name="raw", bufs=BLOCKS * PASSES))
-        grouped_pool = ctx.enter_context(tc.tile_pool(name="grouped", bufs=4))
-        codes_pool = ctx.enter_context(tc.tile_pool(name="codes", bufs=4))
+        grouped_pool = ctx.enter_context(tc.tile_pool(name="grouped", bufs=6))
+        codes_pool = ctx.enter_context(tc.tile_pool(name="codes", bufs=6))
         psum = ctx.enter_context(tc.psum_pool(name="psum", bufs=1))
 
         def bank(index, shape, name):
@@ -64,24 +65,79 @@ def tile_multiheadlatentattention_pb_kernel(tc, x, freq_cis, Wq, out):
         )
         nc.vector.tensor_copy(out=negsin_cos[:, :, :, 1:2], in_=freq_raw[:, :, :, 0:1])
 
+        units = [(0, kind, g) for g in range(PASSES) for kind in (ROTATED, KEPT)]
+        for b in range(1, BLOCKS):
+            units += [(b, kind, g) for kind in (ROTATED, KEPT) for g in range(PASSES)]
+        complete = {}
+        for n in range(UNITS):
+            b, kind, g = units[n]
+            if g == PASSES - 1:
+                complete[b, kind] = n
+
         x_codes = keep.tile([P, TOK_TILES, PASSES * P], U32, name="x_codes", align_bytes=64)
         x_scales = keep.tile([P, TOK_TILES, PASSES * P], U8, name="x_scales", align_bytes=64)
+        rot_shape = [P, BLOCK_HEADS, PAIRS, 2]
         w_raw = {}
+        w_grouped = {}
+        w_codes = {}
+        w_scales = {}
+        acc = {}
+        stage = {}
+
+        def load_weights(b, g):
+            w_raw[b, g] = raw_pool.tile([P, PACK, BLOCK], BF16, name="w_raw")
+            for u in range(2):
+                first = K_PASS * g + 2 * P * u
+                rows = Wq[first : first + 2 * P, BLOCK * b : BLOCK * (b + 1)]
+                nc.sync.dma_start(
+                    out=w_raw[b, g][:, 2 * u : 2 * u + 2, :],
+                    in_=rows.rearrange("(q e) c -> q e c", e=2),
+                )
+
+        def regroup(n):
+            b, kind, g = units[n]
+            w_grouped[n] = grouped_pool.tile(
+                [P, BANK, PACK], BF16, name="w_grouped", align_bytes=64
+            )
+            src = w_raw[b, g][:].rearrange(
+                "p t (h s c i) -> p s h c t i", h=BLOCK_HEADS, s=2, i=4
+            )[:, 1 if kind == ROTATED else 0]
+            dst = w_grouped[n][:].rearrange("p (h c i) t -> p h c t i", h=BLOCK_HEADS, i=4)
+            split = BLOCK_HEADS - VECTOR_HEADS[kind]
+            nc.scalar.copy(out=dst[:, :split], in_=src[:, :split])
+            nc.vector.tensor_copy(out=dst[:, split:], in_=src[:, split:])
+
+        def quantise(n):
+            w_codes[n] = codes_pool.tile([P, BANK], U32, name="w_codes", align_bytes=64)
+            w_scales[n] = codes_pool.tile([P, BANK], U8, name="w_scales", align_bytes=64)
+            nc.vector.quantize_mx(
+                out=w_codes[n][:].bitcast(FP8X4),
+                scales=w_scales[n][:],
+                in_=w_grouped[n][:].rearrange("p w t -> p (w t)"),
+            )
+
+        def multiply(n):
+            b, kind, g = units[n]
+            for tt in range(TOK_TILES):
+                if g == 0:
+                    acc[b, kind, tt] = bank(TOK_TILES * kind + tt, [P, BANK], "acc")
+                nc.tensor.matmul_mx(
+                    out=acc[b, kind, tt][:],
+                    lhsT=x_codes[:, tt, P * g : P * (g + 1)].bitcast(FP8X4),
+                    lhsT_scale=x_scales[:, tt, P * g : P * (g + 1)],
+                    rhs=w_codes[n][:].bitcast(FP8X4),
+                    rhs_scale=w_scales[n][:],
+                    start=(g == 0),
+                    stop=(g == PASSES - 1),
+                )
+
         with tc.tile_pool(name="x", bufs=TOK_TILES) as x_pool:
             x_raw = [x_pool.tile([P, K], BF16, name="x_raw") for tt in range(TOK_TILES)]
             for tt in range(TOK_TILES):
                 nc.sync.dma_start(out=x_raw[tt][:], in_=x_tiles[tt])
-
             for b in range(BLOCKS):
                 for g in range(PASSES):
-                    w_raw[b, g] = raw_pool.tile([P, PACK, BLOCK], BF16, name="w_raw")
-                    for u in range(2):
-                        first = K_PASS * g + 2 * P * u
-                        rows = Wq[first : first + 2 * P, BLOCK * b : BLOCK * (b + 1)]
-                        nc.sync.dma_start(
-                            out=w_raw[b, g][:, 2 * u : 2 * u + 2, :],
-                            in_=rows.rearrange("(q e) c -> q e c", e=2),
-                        )
+                    load_weights(b, g)
 
             for tt in range(TOK_TILES):
                 x_words = x_raw[tt][:].bitcast(F32)
@@ -110,56 +166,11 @@ def tile_multiheadlatentattention_pb_kernel(tc, x, freq_cis, Wq, out):
 
         stage_pool = ctx.enter_context(tc.tile_pool(name="stage", bufs=2 * TOK_TILES))
         rope_pool = ctx.enter_context(tc.tile_pool(name="rope", bufs=3))
-        rot_shape = [P, BLOCK_HEADS, PAIRS, 2]
-        w_grouped = {}
-        w_codes = {}
-        w_scales = {}
-        acc = {}
-        stage = {}
 
-        def regroup(n):
-            group, g = divmod(n, PASSES)
-            b, kind = divmod(group, 2)
-            w_grouped[n] = grouped_pool.tile(
-                [P, BANK, PACK], BF16, name="w_grouped", align_bytes=64
-            )
-            src = w_raw[b, g][:].rearrange(
-                "p t (h s c i) -> p s h c t i", h=BLOCK_HEADS, s=2, i=4
-            )[:, 1 if kind == ROTATED else 0]
-            dst = w_grouped[n][:].rearrange("p (h c i) t -> p h c t i", h=BLOCK_HEADS, i=4)
-            split = BLOCK_HEADS - VECTOR_HEADS[kind]
-            nc.scalar.copy(out=dst[:, :split], in_=src[:, :split])
-            nc.vector.tensor_copy(out=dst[:, split:], in_=src[:, split:])
-
-        def quantise(n):
-            w_codes[n] = codes_pool.tile([P, BANK], U32, name="w_codes", align_bytes=64)
-            w_scales[n] = codes_pool.tile([P, BANK], U8, name="w_scales", align_bytes=64)
-            nc.vector.quantize_mx(
-                out=w_codes[n][:].bitcast(FP8X4),
-                scales=w_scales[n][:],
-                in_=w_grouped[n][:].rearrange("p w t -> p (w t)"),
-            )
-
-        def multiply(n):
-            group, g = divmod(n, PASSES)
-            for tt in range(TOK_TILES):
-                if g == 0:
-                    acc[group, tt] = bank(TOK_TILES * (group % 2) + tt, [P, BANK], "acc")
-                nc.tensor.matmul_mx(
-                    out=acc[group, tt][:],
-                    lhsT=x_codes[:, tt, P * g : P * (g + 1)].bitcast(FP8X4),
-                    lhsT_scale=x_scales[:, tt, P * g : P * (g + 1)],
-                    rhs=w_codes[n][:].bitcast(FP8X4),
-                    rhs_scale=w_scales[n][:],
-                    start=(g == 0),
-                    stop=(g == PASSES - 1),
-                )
-
-        def evacuate(group, tt):
-            b, kind = divmod(group, 2)
+        def evacuate(b, kind, tt):
             if kind == ROTATED:
                 stage[b, tt] = stage_pool.tile([P, BLOCK_HEADS, 2, HALF], F32, name="stage")
-                pairs = acc[group, tt][:].rearrange(
+                pairs = acc[b, kind, tt][:].rearrange(
                     "p (h i two) -> p h i two", h=BLOCK_HEADS, two=2
                 )
                 from_even = rope_pool.tile(rot_shape, F32, name="from_even")
@@ -185,20 +196,28 @@ def tile_multiheadlatentattention_pb_kernel(tc, x, freq_cis, Wq, out):
             else:
                 nc.scalar.copy(
                     out=stage[b, tt][:, :, 0, :],
-                    in_=acc[group, tt][:].rearrange("p (h f) -> p h f", h=BLOCK_HEADS),
+                    in_=acc[b, kind, tt][:].rearrange("p (h f) -> p h f", h=BLOCK_HEADS),
                 )
                 nc.sync.dma_start(
                     out=out_tiles[tt][:, BLOCK * b : BLOCK * (b + 1)],
                     in_=stage[b, tt][:].rearrange("p h s f -> p (h s f)"),
                 )
 
+        tiles = [
+            (b, kind, tt)
+            for b in range(BLOCKS)
+            for kind in (ROTATED, KEPT)
+            for tt in range(TOK_TILES)
+        ]
+        left = 0
         regroup(0)
         for n in range(UNITS):
             if n + 1 < UNITS:
                 regroup(n + 1)
             quantise(n)
-            if n >= PASSES:
-                evacuate(n // PASSES - 1, n % PASSES)
+            while left + LEAVE_LAG <= n and complete[tiles[left][:2]] < n:
+                evacuate(*tiles[left])
+                left += 1
             multiply(n)
-        for tt in range(TOK_TILES):
-            evacuate(GROUPS - 1, tt)
+        for b, kind, tt in tiles[left:]:
+            evacuate(b, kind, tt)

@@ -31,6 +31,7 @@ ROTATED, KEPT = 0, 1
 GROUPS = 2 * BLOCKS
 UNITS = GROUPS * PASSES
 LEAVE_LAG = PASSES + 1
+PACED_BLOCKS = 2
 VECTOR_HEADS = {ROTATED: 2, KEPT: 1}
 
 
@@ -65,9 +66,12 @@ def tile_multiheadlatentattention_pb_kernel(tc, x, freq_cis, Wq, out):
         )
         nc.vector.tensor_copy(out=negsin_cos[:, :, :, 1:2], in_=freq_raw[:, :, :, 0:1])
 
-        units = [(0, kind, g) for g in range(PASSES) for kind in (ROTATED, KEPT)]
-        for b in range(1, BLOCKS):
-            units += [(b, kind, g) for kind in (ROTATED, KEPT) for g in range(PASSES)]
+        units = []
+        for b in range(BLOCKS):
+            if b < PACED_BLOCKS:
+                units += [(b, kind, g) for g in range(PASSES) for kind in (ROTATED, KEPT)]
+            else:
+                units += [(b, kind, g) for kind in (ROTATED, KEPT) for g in range(PASSES)]
         complete = {}
         for n in range(UNITS):
             b, kind, g = units[n]
@@ -215,9 +219,15 @@ def tile_multiheadlatentattention_pb_kernel(tc, x, freq_cis, Wq, out):
             if n + 1 < UNITS:
                 regroup(n + 1)
             quantise(n)
-            while left + LEAVE_LAG <= n and complete[tiles[left][:2]] < n:
-                evacuate(*tiles[left])
-                left += 1
+            b, kind, g = units[n]
+            due = left
+            while due + LEAVE_LAG <= n and complete[tiles[due][:2]] < n:
+                due += 1
+            if g == 0 and b > 0:
+                due = max(due, tiles.index((b - 1, kind, TOK_TILES - 1)) + 1)
+            for tile in tiles[left:due]:
+                evacuate(*tile)
+            left = due
             multiply(n)
         for b, kind, tt in tiles[left:]:
             evacuate(b, kind, tt)

from contextlib import ExitStack

import concourse.mybir as mybir
from concourse.masks import make_identity

FLOPS = 2 * 512 * 2048 * 4096

BF16 = mybir.dt.bfloat16
F32 = mybir.dt.float32
U32 = mybir.dt.uint32
U8 = mybir.dt.uint8
FP8X4 = mybir.dt.float8_e4m3fn_x4
MULT = mybir.AluOpType.mult
ADD = mybir.AluOpType.add

P = 128
PACK = 4
K_PASS = P * PACK
TOKENS = 512
K = 2048
PASSES = K // K_PASS
TOK_TILES = TOKENS // P
HEAD = 256
HALF = 128
PAIRS = HALF // 2
BLOCK_HEADS = 4
BLOCK = BLOCK_HEADS * HEAD
BANK = BLOCK_HEADS * HALF
BLOCKS = 4096 // BLOCK
ROTATED, KEPT = 0, 1
GROUPS = 2 * BLOCKS
UNITS = GROUPS * PASSES
LEAVE_LAG = PASSES + 1
PACED_BLOCKS = 2
VECTOR_HEADS = {ROTATED: 2, KEPT: 1}


def tile_multiheadlatentattention_pb_kernel(tc, x, freq_cis, Wq, out):
    nc = tc.nc
    x_tiles = x.rearrange("b (tt p) c -> (b tt) p c", p=P)
    out_tiles = out.rearrange("b (tt p) h d -> (b tt) p (h d)", p=P)

    with ExitStack() as ctx:
        ctx.enter_context(tc.manual_schedule())
        keep = ctx.enter_context(tc.tile_pool(name="keep", bufs=1))
        raw_pool = ctx.enter_context(tc.tile_pool(name="raw", bufs=BLOCKS * PASSES))
        grouped_pool = ctx.enter_context(tc.tile_pool(name="grouped", bufs=6))
        codes_pool = ctx.enter_context(tc.tile_pool(name="codes", bufs=6))
        psum = ctx.enter_context(tc.psum_pool(name="psum", bufs=1))

        def bank(index, shape, name):
            return psum.tile(shape, F32, name=name, tag="bank%d" % index)

        ident = keep.tile([P, P], F32, name="ident")
        make_identity(nc, ident[:])

        freq_raw = keep.tile([P, TOK_TILES, PAIRS, 2], BF16, name="freq_raw")
        nc.scalar.dma_start(
            out=freq_raw[:], in_=freq_cis.rearrange("(tt p) i two -> p tt i two", p=P)
        )
        cos_sin = keep.tile([P, TOK_TILES, PAIRS, 2], F32, name="cos_sin")
        negsin_cos = keep.tile([P, TOK_TILES, PAIRS, 2], F32, name="negsin_cos")
        nc.vector.tensor_copy(out=cos_sin[:], in_=freq_raw[:])
        nc.vector.tensor_scalar_mul(
            out=negsin_cos[:, :, :, 0:1], in0=freq_raw[:, :, :, 1:2], scalar1=-1.0
        )
        nc.vector.tensor_copy(out=negsin_cos[:, :, :, 1:2], in_=freq_raw[:, :, :, 0:1])

        units = []
        for b in range(BLOCKS):
            if b < PACED_BLOCKS:
                units += [(b, kind, g) for g in range(PASSES) for kind in (ROTATED, KEPT)]
            else:
                units += [(b, kind, g) for kind in (ROTATED, KEPT) for g in range(PASSES)]
        complete = {}
        for n in range(UNITS):
            b, kind, g = units[n]
            if g == PASSES - 1:
                complete[b, kind] = n

        x_codes = keep.tile([P, TOK_TILES, PASSES * P], U32, name="x_codes", align_bytes=64)
        x_scales = keep.tile([P, TOK_TILES, PASSES * P], U8, name="x_scales", align_bytes=64)
        rot_shape = [P, BLOCK_HEADS, PAIRS, 2]
        w_raw = {}
        w_grouped = {}
        w_codes = {}
        w_scales = {}
        acc = {}
        stage = {}

        def load_weights(b, g):
            w_raw[b, g] = raw_pool.tile([P, PACK, BLOCK], BF16, name="w_raw")
            for u in range(2):
                first = K_PASS * g + 2 * P * u
                rows = Wq[first : first + 2 * P, BLOCK * b : BLOCK * (b + 1)]
                nc.sync.dma_start(
                    out=w_raw[b, g][:, 2 * u : 2 * u + 2, :],
                    in_=rows.rearrange("(q e) c -> q e c", e=2),
                )

        def regroup(n):
            b, kind, g = units[n]
            w_grouped[n] = grouped_pool.tile(
                [P, BANK, PACK], BF16, name="w_grouped", align_bytes=64
            )
            src = w_raw[b, g][:].rearrange(
                "p t (h s c i) -> p s h c t i", h=BLOCK_HEADS, s=2, i=4
            )[:, 1 if kind == ROTATED else 0]
            dst = w_grouped[n][:].rearrange("p (h c i) t -> p h c t i", h=BLOCK_HEADS, i=4)
            split = BLOCK_HEADS - VECTOR_HEADS[kind]
            nc.scalar.copy(out=dst[:, :split], in_=src[:, :split])
            nc.vector.tensor_copy(out=dst[:, split:], in_=src[:, split:])

        def quantise(n):
            w_codes[n] = codes_pool.tile([P, BANK], U32, name="w_codes", align_bytes=64)
            w_scales[n] = codes_pool.tile([P, BANK], U8, name="w_scales", align_bytes=64)
            nc.vector.quantize_mx(
                out=w_codes[n][:].bitcast(FP8X4),
                scales=w_scales[n][:],
                in_=w_grouped[n][:].rearrange("p w t -> p (w t)"),
            )

        def multiply(n):
            b, kind, g = units[n]
            for tt in range(TOK_TILES):
                if g == 0:
                    acc[b, kind, tt] = bank(TOK_TILES * kind + tt, [P, BANK], "acc")
                nc.tensor.matmul_mx(
                    out=acc[b, kind, tt][:],
                    lhsT=x_codes[:, tt, P * g : P * (g + 1)].bitcast(FP8X4),
                    lhsT_scale=x_scales[:, tt, P * g : P * (g + 1)],
                    rhs=w_codes[n][:].bitcast(FP8X4),
                    rhs_scale=w_scales[n][:],
                    start=(g == 0),
                    stop=(g == PASSES - 1),
                )

        with tc.tile_pool(name="x", bufs=TOK_TILES) as x_pool:
            x_raw = [x_pool.tile([P, K], BF16, name="x_raw") for tt in range(TOK_TILES)]
            for tt in range(TOK_TILES):
                nc.sync.dma_start(out=x_raw[tt][:], in_=x_tiles[tt])
            for b in range(BLOCKS):
                for g in range(PASSES):
                    load_weights(b, g)

            for tt in range(TOK_TILES):
                x_words = x_raw[tt][:].bitcast(F32)
                x_grouped = x_pool.tile([P, K], BF16, name="x_grouped", align_bytes=64)
                grouped_words = x_grouped[:].bitcast(F32).rearrange(
                    "p (g r u) -> p g r u", g=PASSES, u=2
                )
                for half in range(2):
                    xt = bank(2 * tt + half, [P, 2, 2, P], "xt")
                    for g2 in range(2):
                        for u in range(2):
                            first = P * (2 * (2 * half + g2) + u)
                            nc.tensor.transpose(
                                xt[:, g2, u, :], x_words[:, first : first + P], ident[:]
                            )
                    copy = nc.scalar.copy if half == 0 else nc.vector.tensor_copy
                    copy(
                        out=grouped_words[:, 2 * half : 2 * half + 2, :, :],
                        in_=xt[:].rearrange("p g u r -> p g r u"),
                    )
                nc.vector.quantize_mx(
                    out=x_codes[:, tt, :].bitcast(FP8X4),
                    scales=x_scales[:, tt, :],
                    in_=x_grouped[:],
                )

        stage_pool = ctx.enter_context(tc.tile_pool(name="stage", bufs=2 * TOK_TILES))
        rope_pool = ctx.enter_context(tc.tile_pool(name="rope", bufs=3))

        def evacuate(b, kind, tt):
            if kind == ROTATED:
                stage[b, tt] = stage_pool.tile([P, BLOCK_HEADS, 2, HALF], F32, name="stage")
                pairs = acc[b, kind, tt][:].rearrange(
                    "p (h i two) -> p h i two", h=BLOCK_HEADS, two=2
                )
                from_even = rope_pool.tile(rot_shape, F32, name="from_even")
                from_odd = rope_pool.tile(rot_shape, F32, name="from_odd")
                nc.vector.tensor_tensor(
                    out=from_even[:],
                    in0=pairs[:, :, :, 0:1].to_broadcast(rot_shape),
                    in1=cos_sin[:, tt : tt + 1, :, :].to_broadcast(rot_shape),
                    op=MULT,
                )
                nc.vector.tensor_tensor(
                    out=from_odd[:],
                    in0=pairs[:, :, :, 1:2].to_broadcast(rot_shape),
                    in1=negsin_cos[:, tt : tt + 1, :, :].to_broadcast(rot_shape),
                    op=MULT,
                )
                nc.gpsimd.tensor_tensor(
                    out=stage[b, tt][:, :, 1, :],
                    in0=from_even[:].rearrange("p h i two -> p h (i two)"),
                    in1=from_odd[:].rearrange("p h i two -> p h (i two)"),
                    op=ADD,
                )
            else:
                nc.scalar.copy(
                    out=stage[b, tt][:, :, 0, :],
                    in_=acc[b, kind, tt][:].rearrange("p (h f) -> p h f", h=BLOCK_HEADS),
                )
                nc.sync.dma_start(
                    out=out_tiles[tt][:, BLOCK * b : BLOCK * (b + 1)],
                    in_=stage[b, tt][:].rearrange("p h s f -> p (h s f)"),
                )

        tiles = [
            (b, kind, tt)
            for b in range(BLOCKS)
            for kind in (ROTATED, KEPT)
            for tt in range(TOK_TILES)
        ]
        left = 0
        regroup(0)
        for n in range(UNITS):
            if n + 1 < UNITS:
                regroup(n + 1)
            quantise(n)
            b, kind, g = units[n]
            due = left
            while due + LEAVE_LAG <= n and complete[tiles[due][:2]] < n:
                due += 1
            if g == 0 and b > 0:
                due = max(due, tiles.index((b - 1, kind, TOK_TILES - 1)) + 1)
            for tile in tiles[left:due]:
                evacuate(*tile)
            left = due
            multiply(n)
        for b, kind, tt in tiles[left:]:
            evacuate(b, kind, tt)
